import numpy as np
import ml_dtypes


def mxq(x, axis, fmt="e4m3"):
    dtype, down = {"e4m3": (ml_dtypes.float8_e4m3fn, 7), "e5m2": (ml_dtypes.float8_e5m2, 14)}[fmt]
    v = np.moveaxis(np.asarray(x, np.float32).astype(ml_dtypes.bfloat16).astype(np.float64), axis, -1)
    blocks = v.reshape(v.shape[:-1] + (-1, 32))
    amax = np.abs(blocks).max(-1, keepdims=True)
    byte = np.maximum(np.where(amax > 0, np.frexp(amax)[1] - 1 + 127, 0) - down, 1)
    scale = np.exp2(byte - 127.0)
    codes = (blocks / scale).astype(np.float32).astype(dtype).astype(np.float64)
    return np.moveaxis((codes * scale).reshape(v.shape), -1, axis)


WIDE = False


def mx_kscale(k):
    if not WIDE:
        return np.ones(k)
    levels = np.array([18, -18])
    if k % 512:
        return np.exp2(np.random.permutation(np.resize(levels, k // 32))).repeat(32)
    a = np.empty((k // 512, 16))
    for p in range(k // 512):
        a[p, :8] = np.random.permutation(np.resize(levels, 8))
        for g in range(8):
            far = levels[np.abs(levels - a[p, g]) >= 10]
            a[p, g + 8] = far[np.random.randint(len(far))]
    return np.exp2(a.ravel()).repeat(32)


BF16 = ml_dtypes.bfloat16


def bf(x):
    return np.asarray(x, np.float32).astype(BF16)


def f64(x):
    return np.asarray(x).astype(np.float64)


B, C, V, K, OUT = 4, 128, 2048, 4, 512


def setup_inputs():
    s = mx_kscale(B * V)
    s = (s / np.min(s)).reshape(B, V)
    u = mx_kscale(OUT)
    st = np.tile(s.T, (1, C))
    g = np.random.standard_normal((V, V))
    lap = bf((g + g.T) * (0.45 / np.sqrt(V)))
    input0 = bf(np.random.standard_normal((B, C, V)))
    x10 = bf(np.random.standard_normal((V, C * B)) * 0.64)
    x20 = bf(np.random.standard_normal((V, C * B)) * 0.83)
    weight0 = bf(np.random.standard_normal((OUT, C * K)) / np.sqrt(C * K))
    bias = bf(np.random.standard_normal(OUT) * 0.2)
    x3 = 2.0 * (f64(lap) @ f64(x20)) - f64(x10)
    go = bf(np.random.standard_normal((B, OUT, V)) * np.exp2(np.random.randint(-6, 1, (B, 1, V)))
            / s[:, None, :] * u[None, :, None])
    return {"input": bf(f64(input0) * s[:, None, :]),
            "x1": bf(f64(x10) * st),
            "x2": bf(f64(x20) * st),
            "laplacian": lap,
            "weight": bf(f64(weight0) / u[:, None]),
            "bias": bias,
            "x3": np.asarray(x3, np.float32),
            "grad_out": go}


def reference(input, x1, x2, laplacian, weight, bias, x3, grad_out):
    dz = f64(grad_out).transpose(0, 2, 1).reshape(B * V, OUT)
    wk0 = f64(weight).reshape(OUT, C, K)[:, :, 0]
    dx = mxq(dz, 1, "e5m2") @ mxq(wk0, 0, "e4m3")
    dinput = dx.reshape(B, V, C).transpose(0, 2, 1)
    x0 = f64(input).transpose(2, 1, 0).reshape(V, C * B)
    f = np.stack([x0, f64(x1), f64(x2), f64(x3)], axis=0)
    f = f.reshape(K, V, C, B).transpose(3, 1, 2, 0).reshape(B * V, C * K)
    dw = mxq(dz, 0, "e5m2").T @ mxq(f, 0, "e4m3")
    return dinput, dw

@@ -1,0 +1,341 @@
+from contextlib import ExitStack
+
+import concourse.mybir as mybir
+from concourse.masks import make_identity
+
+B, C, V, K, OUT = 4, 128, 2048, 4, 512
+FLOPS = 2 * B * V * OUT * C + 2 * B * V * OUT * C * K
+BYTES = 2 * (B * C * V + 2 * V * C * B + OUT * C * K + B * OUT * V) + 4 * (V * C * B + B * C * V + OUT * C * K)
+
+F32 = mybir.dt.float32
+BF16 = mybir.dt.bfloat16
+U32 = mybir.dt.uint32
+U8 = mybir.dt.uint8
+E4M3 = mybir.dt.float8_e4m3fn_x4
+E5M2 = mybir.dt.float8_e5m2_x4
+
+P = 128
+PACK = 4
+PASS = P * PACK
+GROUPS = V // PASS
+UNITS = B * GROUPS
+PAIRS = UNITS // 2
+
+X_START = 1
+CATCH_UP = (9, 12)
+F_DEFER = 3
+W_STEP = 4
+FEAT_BUFS = 5
+TOK_BUFS = 7
+V_SHARE = {2: (1, 2), 3: (1,), 4: (1,), 5: (1,), 6: (1, 2), 7: (1, 2)}
+ORDER0 = [(2, 0), (2, 1), (1, 0), (3, 0), (1, 1), (3, 1)]
+ORDER = [(2, 0), (1, 0), (3, 0), (2, 1), (1, 1), (3, 1)]
+X_NUM, X_OFF, X_DEN = 7, 6, 12
+X0_STEP = 4
+STORE_STEP = 11
+Q_LAG = 2
+Q_ODD = 1
+M_LAG = 3
+HALVES = True
+GI_S = ()
+OUT1_V = False
+X_BUFS = 2
+FP_BUFS = 4
+GO_BUFS = 8
+FQ_BUFS = 4
+LOADS = [("go", 0, 0), ("x", 2, 0), ("go", 1, 0), ("x", 1, 0), ("go", 2, 0), ("go", 3, 0), ("x", 3, 0), ("x0", 0, 0), ("go", 0, 1), "w",
+         ("x0", 1, 0), ("go", 1, 1), ("x", 2, 1), ("x", 1, 1), ("go", 2, 1), ("x", 3, 1), ("go", 3, 1)]
+
+
+def dz_bg(n):
+    return n % B, n // B
+
+
+def x_step(i):
+    return X_START + i - sum(1 for c in CATCH_UP if i >= c)
+
+
+def tile_graph_conv_pb_v_kernel(tc, x0, x1, x2, laplacian, weight, bias, x3, grad_out, out_0, out_1):
+    nc = tc.nc
+    with ExitStack() as ctx:
+        keep = ctx.enter_context(tc.tile_pool(name="keep", bufs=1))
+        loads = ctx.enter_context(tc.tile_pool(name="loads", bufs=2))
+        work = ctx.enter_context(tc.tile_pool(name="work", bufs=2))
+        psum = ctx.enter_context(tc.psum_pool(name="psum", bufs=1))
+        ctx.enter_context(tc.manual_schedule(engines={mybir.EngineType.SP}))
+
+        ident = keep.tile([P, P], F32, name="ident")
+        make_identity(nc, ident[:])
+
+        go, xs, x0s = {}, {}, {}
+
+        def load_go_unit(b, g):
+            t = loads.tile([P, PACK, PASS], BF16, name="go_unit", tag="go_unit", bufs=GO_BUFS, align_bytes=64)
+            src = grad_out[b].rearrange("(p j) v -> p j v", j=PACK)
+            nc.sync.dma_start(out=t[:], in_=src[:, :, g * PASS:(g + 1) * PASS])
+            go[b, g] = t[:]
+
+        def load_go_half(b, half):
+            t = loads.tile([P, PACK, 2 * PASS], BF16, name="go_half", bufs=4, align_bytes=64)
+            src = grad_out[b].rearrange("(p j) v -> p j v", j=PACK)
+            nc.sync.dma_start(out=t[:], in_=src[:, :, 2 * half * PASS:2 * (half + 1) * PASS])
+            go[b, 2 * half] = t[:, :, 0:PASS]
+            go[b, 2 * half + 1] = t[:, :, PASS:2 * PASS]
+
+        def load_x(k, g):
+            src = (x1, x2, x3)[k - 1]
+            t = loads.tile([P, PACK, C * B], F32 if k == 3 else BF16, name="x%d" % k, bufs=X_BUFS, align_bytes=64)
+            nc.sync.dma_start(out=t[:], in_=src[g * PASS:(g + 1) * PASS, :].rearrange("(p j) w -> p j w", j=PACK))
+            xs[k, g] = t[:]
+
+        def load_x0(bh, half):
+            t = loads.tile([P, 2, 2 * PASS], BF16, name="x0", tag="x0", bufs=4, align_bytes=64)
+            src = x0[2 * bh:2 * bh + 2, :, 2 * half * PASS:2 * (half + 1) * PASS]
+            nc.sync.dma_start(out=t[:], in_=src.rearrange("b c v -> c b v"))
+            x0s[bh, half] = t[:]
+
+        w_raw = keep.tile([P, PACK, C * K], BF16, name="w_raw")
+        w_grouped = keep.tile([P, C, PACK], BF16, name="w_grouped", align_bytes=64)
+        w_codes = keep.tile([P, C], U32, name="w_codes", align_bytes=64)
+        w_scales = keep.tile([P, C], U8, name="w_scales", align_bytes=64)
+
+        def load_w():
+            nc.sync.dma_start(out=w_raw[:], in_=weight.rearrange("(p j) w -> p j w", j=PACK))
+
+        def group_w():
+            src = w_raw[:].rearrange("p j (c k) -> p k c j", k=K)
+            nc.vector.tensor_copy(out=w_grouped[:], in_=src[:, 0])
+
+        def quantize_w():
+            nc.vector.quantize_mx(out=w_codes[:].bitcast(E4M3), scales=w_scales[:],
+                                  in_=w_grouped[:].rearrange("p c j -> p (c j)"))
+
+        acc = [psum.tile([P, PASS], F32, name="acc%d" % j) for j in range(PACK)]
+
+        feat, feat_q, tok, tok_q, f_pair, f_q, banks, staged = {}, {}, {}, {}, {}, {}, {}, {}
+
+        def group_feat(n):
+            t = work.tile([P, PASS, PACK], BF16, name="feat", bufs=2, align_bytes=64)
+            dst = t[:].rearrange("p (h c i) t -> p h c t i", h=2, i=4)
+            src = go[dz_bg(n)].rearrange("p t (h c i) -> p h c t i", h=2, i=4)
+            if n in GI_S:
+                nc.vector.tensor_copy(out=dst[:, 0], in_=src[:, 0])
+                nc.scalar.copy(out=dst[:, 1], in_=src[:, 1])
+            else:
+                nc.vector.tensor_copy(out=t[:].rearrange("p (c i) t -> p c t i", i=4),
+                                      in_=go[dz_bg(n)].rearrange("p t (c i) -> p c t i", i=4))
+            feat[n] = t[:]
+
+        def quantize(src, fmt, name, bufs):
+            codes = work.tile([P, PASS], U32, name=name + "_codes", bufs=bufs, align_bytes=64)
+            scales = work.tile([P, PASS], U8, name=name + "_scales", bufs=bufs, align_bytes=64)
+            nc.vector.quantize_mx(out=codes[:].bitcast(fmt), scales=scales[:], in_=src)
+            return codes[:], scales[:]
+
+        def quantize_feat(n):
+            feat_q[n] = quantize(feat[n].rearrange("p v j -> p (v j)"), E5M2, "feat", FEAT_BUFS)
+
+        def matmul_out0(n):
+            bank = psum.tile([P, PASS], F32, name="bank_out0")
+            codes, scales = feat_q[n]
+            nc.tensor.matmul_mx(out=bank[:], lhsT=w_codes[:].bitcast(E4M3), lhsT_scale=w_scales[:],
+                                rhs=codes.bitcast(E5M2), rhs_scale=scales, start=True, stop=True)
+            banks["out0", n] = bank[:]
+
+        def empty_out0(n):
+            b, g = dz_bg(n)
+            if g != 1:
+                if g == 0:
+                    t = keep.tile([P, 2 * PASS], F32, name="staged_%d" % b)
+                else:
+                    t = loads.tile([P, PASS], F32, name="staged_late", tag="go_unit", bufs=GO_BUFS, align_bytes=64)
+                staged[b, g] = t[:]
+            dst = staged[b, 0][:, g * PASS:(g + 1) * PASS] if g < 2 else staged[b, g]
+            nc.scalar.copy(out=dst, in_=banks["out0", n])
+
+        def store_out0(b, g):
+            width = 2 * PASS if g == 0 else PASS
+            nc.sync.dma_start(out=out_0[b, :, g * PASS:g * PASS + width], in_=staged[b, g])
+
+        def transpose_tok(n, jh):
+            bank = psum.tile([P, 2, 2, P], F32, name="bank_tok%d" % jh)
+            words = go[dz_bg(n)].bitcast(F32)
+            for jl in range(2):
+                for u in range(2):
+                    nc.tensor.transpose(bank[:, jl, u, :], words[:, 2 * jh + jl, u:PASS // 2:2], ident[:])
+            banks["tok", n, jh] = bank[:]
+
+        def empty_tok(n, jh):
+            if jh == 0:
+                t = work.tile([P, 2, PASS], F32, name="tok", bufs=2, align_bytes=64)
+                tok[n] = t[:]
+            nc.scalar.copy(out=tok[n][:, jh, :].rearrange("p (j r u) -> p j r u", j=2, u=2),
+                           in_=banks["tok", n, jh].rearrange("p j u r -> p j r u"))
+
+        def quantize_tok(n):
+            tok_q[dz_bg(n)] = quantize(tok[n].rearrange("p h w -> p (h w)").bitcast(BF16), E5M2, "tok", TOK_BUFS)
+
+        def pair_tile(q):
+            if q not in f_pair:
+                t = work.tile([P, 2 * K * C * PACK], BF16, name="f_pair", bufs=FP_BUFS, align_bytes=64)
+                f_pair[q] = t[:]
+            return f_pair[q]
+
+        def transpose_x0(q):
+            g, bh = divmod(q, 2)
+            bank = psum.tile([P, 2, 2, P], F32, name="bank_x0")
+            words = x0s[bh, g // 2][:, :, (g % 2) * PASS:(g % 2 + 1) * PASS].bitcast(F32)
+            for bl in range(2):
+                for u in range(2):
+                    nc.tensor.transpose(bank[:, bl, u, :], words[:, bl, u:PASS // 2:2], ident[:])
+            banks["x0", q] = bank[:]
+
+        def empty_x0(q):
+            dst = pair_tile(q).bitcast(F32).rearrange("p (bl k c u) -> p k bl c u", bl=2, k=K, u=2)
+            nc.scalar.copy(out=dst[:, 0], in_=banks["x0", q].rearrange("p bl u c -> p bl c u"))
+
+        def group_x(q, k):
+            g, bh = divmod(q, 2)
+            if k == 3:
+                dst = pair_tile(q).rearrange("p (bl k c t) -> p k c t bl", bl=2, k=K, t=PACK)
+                src = xs[k, g].rearrange("p j (c bh bl) -> p bh c j bl", bh=2, bl=2)
+            else:
+                dst = pair_tile(q).rearrange("p (bl k c i t) -> p k c t i bl", bl=2, k=K, i=2, t=PACK)
+                src = xs[k, g].rearrange("p j (c i bh bl) -> p bh c j i bl", i=2, bh=2, bl=2)
+            if k in V_SHARE.get(q, ()):
+                nc.vector.tensor_copy(out=dst[:, k], in_=src[:, bh])
+            else:
+                nc.scalar.copy(out=dst[:, k], in_=src[:, bh])
+
+        def quantize_f(n):
+            width = K * C * PACK
+            f_q[n] = quantize(f_pair[n // 2][:, (n % 2) * width:(n % 2 + 1) * width], E4M3, "f", FQ_BUFS)
+
+        def matmul_out1(n):
+            dz_codes, dz_scales = tok_q[n % B, n // B]
+            f_codes, f_scales = f_q[n]
+            for j in range(PACK):
+                cols = slice(j * P, (j + 1) * P)
+                nc.tensor.matmul_mx(out=acc[j][:], lhsT=dz_codes[:, cols].bitcast(E5M2), lhsT_scale=dz_scales[:, cols],
+                                    rhs=f_codes.bitcast(E4M3), rhs_scale=f_scales,
+                                    start=(n == 0), stop=(n == UNITS - 1))
+
+        def finish_out1():
+            rows = out_1.rearrange("(p j) w -> p j w", j=PACK)
+            for jh in range(2):
+                t = loads.tile([P, 2, C, K], F32, name="dw", tag="x0", bufs=4, align_bytes=64)
+                for jl in range(2):
+                    src = acc[2 * jh + jl][:].rearrange("p (k c) -> p c k", k=K)
+                    if jl == 0 and OUT1_V:
+                        nc.vector.tensor_copy(out=t[:, jl], in_=src)
+                    else:
+                        nc.scalar.copy(out=t[:, jl], in_=src)
+                nc.sync.dma_start(out=rows[:, 2 * jh:2 * jh + 2, :], in_=t[:].rearrange("p j c k -> p j (c k)"))
+
+        def ok(n, count=UNITS):
+            return 0 <= n < count
+
+        def load(item):
+            if item == "w":
+                load_w()
+            elif item[0] == "go":
+                load_go_unit(item[1], item[2])
+            elif item[0] == "goh":
+                load_go_half(item[1], item[2])
+            elif item[0] == "x0":
+                load_x0(item[1], item[2])
+            else:
+                load_x(item[1], item[2])
+
+        for item in LOADS:
+            load(item)
+
+        def go_late(b, g):
+            if HALVES:
+                if g == 2:
+                    load_go_half(b, 1)
+            else:
+                load_go_unit(b, g)
+
+        pieces = []
+        for g in range(GROUPS):
+            order = ORDER0 if g == 0 else ORDER
+            pieces.extend((2 * g + bh, k) for k, bh in order)
+        piece_step = {pc: (j * X_NUM + X_OFF) // X_DEN for j, pc in enumerate(pieces)}
+        done = {q: max(piece_step[q, k] for k in (1, 2, 3)) for q in range(PAIRS)}
+        done[0] = max(done[0], X0_STEP)
+        done[1] = max(done[1], X0_STEP)
+        qf_step = {n: done[n // 2] + 1 + Q_ODD * (n % 2) for n in range(UNITS)}
+        mm_step = {n: max(qf_step[n] + 1, n + 2) for n in range(UNITS)}
+        feat_step = {n: n + (F_DEFER if n >= UNITS - F_DEFER else 0) for n in range(UNITS)}
+        out0_step = {n: max(feat_step[n] + 1, W_STEP + 1 + n // 2) for n in range(UNITS)}
+        last = max(max(out0_step.values()), max(mm_step.values()))
+
+        def at(table, s):
+            return [key for key in table if table[key] == s]
+
+        for s in range(last + 1):
+            outs = at(out0_step, s)
+            if ok(s):
+                transpose_tok(s, 0)
+                transpose_tok(s, 1)
+            for q in at(done, s):
+                if q % 2 == 0 or q - 1 not in at(done, s):
+                    transpose_x0(q)
+            for n in outs[:1]:
+                matmul_out0(n)
+            for n in at(mm_step, s):
+                matmul_out1(n)
+            for n in at(feat_step, s):
+                group_feat(n)
+            if ok(s):
+                empty_tok(s, 0)
+                empty_tok(s, 1)
+            for n in outs[:1]:
+                empty_out0(n)
+            for n in outs[1:]:
+                matmul_out0(n)
+            if ok(s - 1):
+                quantize_tok(s - 1)
+            if s == W_STEP:
+                group_w()
+            for n in at(feat_step, s):
+                quantize_feat(n)
+            if s == W_STEP:
+                quantize_w()
+            for n in at(qf_step, s):
+                quantize_f(n)
+            for q in at(done, s):
+                if not (q % 2 == 0 or q - 1 not in at(done, s)):
+                    transpose_x0(q)
+                empty_x0(q)
+            for q, k in at(piece_step, s):
+                group_x(q, k)
+            for n in outs[1:]:
+                empty_out0(n)
+            if s == done[1]:
+                go_late(0, 2)
+                load_x(2, 2)
+                load_x(1, 2)
+                go_late(1, 2)
+                load_x0(0, 1)
+                load_x(3, 2)
+                go_late(2, 2)
+                load_x0(1, 1)
+                go_late(3, 2)
+            if s == done[3]:
+                load_x(2, 3)
+                go_late(0, 3)
+                load_x(1, 3)
+                load_x(3, 3)
+                go_late(1, 3)
+                go_late(2, 3)
+                go_late(3, 3)
+            if s == STORE_STEP:
+                for b in range(B):
+                    store_out0(b, 0)
+            for n in range(UNITS // 2, UNITS):
+                if max(STORE_STEP, out0_step[n]) == s:
+                    store_out0(n % B, n // B)
+            if s == mm_step[UNITS - 1]:
+                finish_out1()

@@ -23,11 +23,11 @@ PAIRS = UNITS // 2
 
 X_START = 1
 CATCH_UP = (9, 12)
-F_DEFER = 3
+F_DEFER = 1
 W_STEP = 4
-FEAT_BUFS = 5
-TOK_BUFS = 7
-V_SHARE = {2: (1, 2), 3: (1,), 4: (1,), 5: (1,), 6: (1, 2), 7: (1, 2)}
+FEAT_BUFS = 6
+TOK_BUFS = 4
+V_SHARE = {q: (1, 3) if q == PAIRS - 1 else (1,) for q in range(PAIRS)}
 ORDER0 = [(2, 0), (2, 1), (1, 0), (3, 0), (1, 1), (3, 1)]
 ORDER = [(2, 0), (1, 0), (3, 0), (2, 1), (1, 1), (3, 1)]
 X_NUM, X_OFF, X_DEN = 7, 6, 12
@@ -37,12 +37,24 @@ Q_LAG = 2
 Q_ODD = 1
 M_LAG = 3
 HALVES = True
+LEAD1 = 9
+LEAD2 = 9
+TIGHT = 0
+X3_FIRST = True
+OUT1_FIRST = False
+X0_BUFS = 4
+M_FIRST = False
+AHEAD = 0
+W_POS = 9
+SPLIT = True
 GI_S = ()
-OUT1_V = False
+OUT1_V = ()
+JOIN = True
+F_SHIFT = 2
 X_BUFS = 2
-FP_BUFS = 4
+FP_BUFS = 3
 GO_BUFS = 8
-FQ_BUFS = 4
+FQ_BUFS = 5
 LOADS = [("go", 0, 0), ("x", 2, 0), ("go", 1, 0), ("x", 1, 0), ("go", 2, 0), ("go", 3, 0), ("x", 3, 0), ("x0", 0, 0), ("go", 0, 1), "w",
          ("x0", 1, 0), ("go", 1, 1), ("x", 2, 1), ("x", 1, 1), ("go", 2, 1), ("x", 3, 1), ("go", 3, 1)]
 
@@ -62,7 +74,7 @@ def tile_graph_conv_pb_v_kernel(tc, x0, x1, x2, laplacian, weight, bias, x3, gra
         loads = ctx.enter_context(tc.tile_pool(name="loads", bufs=2))
         work = ctx.enter_context(tc.tile_pool(name="work", bufs=2))
         psum = ctx.enter_context(tc.psum_pool(name="psum", bufs=1))
-        ctx.enter_context(tc.manual_schedule(engines={mybir.EngineType.SP}))
+        ctx.enter_context(tc.manual_schedule())
 
         ident = keep.tile([P, P], F32, name="ident")
         make_identity(nc, ident[:])
@@ -89,10 +101,16 @@ def tile_graph_conv_pb_v_kernel(tc, x0, x1, x2, laplacian, weight, bias, x3, gra
             xs[k, g] = t[:]
 
         def load_x0(bh, half):
-            t = loads.tile([P, 2, 2 * PASS], BF16, name="x0", tag="x0", bufs=4, align_bytes=64)
+            t = loads.tile([P, 2, 2 * PASS], BF16, name="x0", tag="x0", bufs=2, align_bytes=64)
             src = x0[2 * bh:2 * bh + 2, :, 2 * half * PASS:2 * (half + 1) * PASS]
             nc.sync.dma_start(out=t[:], in_=src.rearrange("b c v -> c b v"))
-            x0s[bh, half] = t[:]
+            x0s[bh, 2 * half] = t[:, :, 0:PASS]
+            x0s[bh, 2 * half + 1] = t[:, :, PASS:2 * PASS]
+
+        def load_x0_pair(bh, g):
+            t = loads.tile([P, 2, PASS], BF16, name="x0p", tag="x0p", bufs=X0_BUFS, align_bytes=64)
+            nc.sync.dma_start(out=t[:], in_=x0[2 * bh:2 * bh + 2, :, g * PASS:(g + 1) * PASS].rearrange("b c v -> c b v"))
+            x0s[bh, g] = t[:]
 
         w_raw = keep.tile([P, PACK, C * K], BF16, name="w_raw")
         w_grouped = keep.tile([P, C, PACK], BF16, name="w_grouped", align_bytes=64)
@@ -136,7 +154,7 @@ def tile_graph_conv_pb_v_kernel(tc, x0, x1, x2, laplacian, weight, bias, x3, gra
             feat_q[n] = quantize(feat[n].rearrange("p v j -> p (v j)"), E5M2, "feat", FEAT_BUFS)
 
         def matmul_out0(n):
-            bank = psum.tile([P, PASS], F32, name="bank_out0")
+            bank = psum.tile([P, PASS], F32, name="bank_out0", tag="bank", bufs=4)
             codes, scales = feat_q[n]
             nc.tensor.matmul_mx(out=bank[:], lhsT=w_codes[:].bitcast(E4M3), lhsT_scale=w_scales[:],
                                 rhs=codes.bitcast(E5M2), rhs_scale=scales, start=True, stop=True)
@@ -158,7 +176,7 @@ def tile_graph_conv_pb_v_kernel(tc, x0, x1, x2, laplacian, weight, bias, x3, gra
             nc.sync.dma_start(out=out_0[b, :, g * PASS:g * PASS + width], in_=staged[b, g])
 
         def transpose_tok(n, jh):
-            bank = psum.tile([P, 2, 2, P], F32, name="bank_tok%d" % jh)
+            bank = psum.tile([P, 2, 2, P], F32, name="bank_tr", tag="bank", bufs=4)
             words = go[dz_bg(n)].bitcast(F32)
             for jl in range(2):
                 for u in range(2):
@@ -183,8 +201,8 @@ def tile_graph_conv_pb_v_kernel(tc, x0, x1, x2, laplacian, weight, bias, x3, gra
 
         def transpose_x0(q):
             g, bh = divmod(q, 2)
-            bank = psum.tile([P, 2, 2, P], F32, name="bank_x0")
-            words = x0s[bh, g // 2][:, :, (g % 2) * PASS:(g % 2 + 1) * PASS].bitcast(F32)
+            bank = psum.tile([P, 2, 2, P], F32, name="bank_tr", tag="bank", bufs=4)
+            words = x0s[bh, g].bitcast(F32)
             for bl in range(2):
                 for u in range(2):
                     nc.tensor.transpose(bank[:, bl, u, :], words[:, bl, u:PASS // 2:2], ident[:])
@@ -211,10 +229,10 @@ def tile_graph_conv_pb_v_kernel(tc, x0, x1, x2, laplacian, weight, bias, x3, gra
             width = K * C * PACK
             f_q[n] = quantize(f_pair[n // 2][:, (n % 2) * width:(n % 2 + 1) * width], E4M3, "f", FQ_BUFS)
 
-        def matmul_out1(n):
+        def matmul_out1(n, js):
             dz_codes, dz_scales = tok_q[n % B, n // B]
             f_codes, f_scales = f_q[n]
-            for j in range(PACK):
+            for j in js:
                 cols = slice(j * P, (j + 1) * P)
                 nc.tensor.matmul_mx(out=acc[j][:], lhsT=dz_codes[:, cols].bitcast(E5M2), lhsT_scale=dz_scales[:, cols],
                                     rhs=f_codes.bitcast(E4M3), rhs_scale=f_scales,
@@ -222,120 +240,119 @@ def tile_graph_conv_pb_v_kernel(tc, x0, x1, x2, laplacian, weight, bias, x3, gra
 
         def finish_out1():
             rows = out_1.rearrange("(p j) w -> p j w", j=PACK)
-            for jh in range(2):
-                t = loads.tile([P, 2, C, K], F32, name="dw", tag="x0", bufs=4, align_bytes=64)
-                for jl in range(2):
-                    src = acc[2 * jh + jl][:].rearrange("p (k c) -> p c k", k=K)
-                    if jl == 0 and OUT1_V:
-                        nc.vector.tensor_copy(out=t[:, jl], in_=src)
-                    else:
-                        nc.scalar.copy(out=t[:, jl], in_=src)
-                nc.sync.dma_start(out=rows[:, 2 * jh:2 * jh + 2, :], in_=t[:].rearrange("p j c k -> p j (c k)"))
+            for j in range(PACK):
+                t = loads.tile([P, C, K], F32, name="dw", tag="x0p", bufs=X0_BUFS, align_bytes=64)
+                src = acc[j][:].rearrange("p (k c) -> p c k", k=K)
+                if j in OUT1_V:
+                    nc.vector.tensor_copy(out=t[:], in_=src)
+                else:
+                    nc.scalar.copy(out=t[:], in_=src)
+                nc.sync.dma_start(out=rows[:, j, :], in_=t[:].rearrange("p c k -> p (c k)"))
 
         def ok(n, count=UNITS):
             return 0 <= n < count
 
-        def load(item):
-            if item == "w":
-                load_w()
-            elif item[0] == "go":
-                load_go_unit(item[1], item[2])
-            elif item[0] == "goh":
-                load_go_half(item[1], item[2])
-            elif item[0] == "x0":
-                load_x0(item[1], item[2])
-            else:
-                load_x(item[1], item[2])
+        def load_group(g):
+            halves = HALVES and g >= 2
+            seq = [("go", 0), ("x", 2), ("x", 1), ("go", 1), ("x", 3), ("x0", 0), ("go", 2), ("go", 3), ("x0", 1)]
+            if g == 0:
+                seq = seq[:W_POS] + [("w", 0)] + seq[W_POS:]
+            for kind, i in seq:
+                if kind == "w":
+                    load_w()
+                elif kind == "x":
+                    load_x(i, g)
+                elif kind == "go":
+                    if not halves:
+                        load_go_unit(i, g)
+                    elif g == 2:
+                        load_go_half(i, 1)
+                elif not halves:
+                    load_x0_pair(i, g)
+                elif g == 2:
+                    load_x0(i, 1)
 
-        for item in LOADS:
-            load(item)
-
-        def go_late(b, g):
-            if HALVES:
-                if g == 2:
-                    load_go_half(b, 1)
-            else:
-                load_go_unit(b, g)
-
-        pieces = []
-        for g in range(GROUPS):
-            order = ORDER0 if g == 0 else ORDER
-            pieces.extend((2 * g + bh, k) for k, bh in order)
-        piece_step = {pc: (j * X_NUM + X_OFF) // X_DEN for j, pc in enumerate(pieces)}
-        done = {q: max(piece_step[q, k] for k in (1, 2, 3)) for q in range(PAIRS)}
-        done[0] = max(done[0], X0_STEP)
-        done[1] = max(done[1], X0_STEP)
-        qf_step = {n: done[n // 2] + 1 + Q_ODD * (n % 2) for n in range(UNITS)}
-        mm_step = {n: max(qf_step[n] + 1, n + 2) for n in range(UNITS)}
-        feat_step = {n: n + (F_DEFER if n >= UNITS - F_DEFER else 0) for n in range(UNITS)}
+        load_group(0)
+        load_group(1)
+        feat_step = {n: n + (F_SHIFT if n >= UNITS - F_DEFER else 0) for n in range(UNITS)}
         out0_step = {n: max(feat_step[n] + 1, W_STEP + 1 + n // 2) for n in range(UNITS)}
+        pair_step = {q: 2 * q - (q >= LEAD1) - (q >= LEAD2) for q in range(PAIRS)}
+        qf_step = {n: pair_step[n // 2] + 2 + n % 2 for n in range(UNITS)}
+        mm_step = {n: max(qf_step[n] + (1 if n >= TIGHT else 0), min(n + M_LAG, UNITS + 1)) for n in range(UNITS)}
+        mm_step[UNITS - 2] = min(mm_step[UNITS - 2], UNITS + 1) if JOIN else mm_step[UNITS - 2]
+        mm_step[UNITS - 1] = min(mm_step[UNITS - 1], UNITS + 1) if JOIN else mm_step[UNITS - 1]
         last = max(max(out0_step.values()), max(mm_step.values()))
 
         def at(table, s):
             return [key for key in table if table[key] == s]
 
         for s in range(last + 1):
-            outs = at(out0_step, s)
+            outs = [n for n in at(out0_step, s) if feat_step[n] < UNITS - F_DEFER]
+            mms = [(n, j) for n in at(mm_step, s) for j in range(PACK)]
+            cut = len(mms) // 2 if SPLIT and ok(s) else 0
+            for n in at(qf_step, s):
+                if mm_step[n] == s:
+                    quantize_f(n)
+            late = s >= UNITS - F_DEFER
+            if s == mm_step[UNITS - 1]:
+                mms = sorted(mms, key=lambda nj: nj[1])
+            for n in at(feat_step, s):
+                if not late:
+                    group_feat(n)
             if ok(s):
                 transpose_tok(s, 0)
-                transpose_tok(s, 1)
-            for q in at(done, s):
-                if q % 2 == 0 or q - 1 not in at(done, s):
-                    transpose_x0(q)
-            for n in outs[:1]:
-                matmul_out0(n)
-            for n in at(mm_step, s):
-                matmul_out1(n)
-            for n in at(feat_step, s):
-                group_feat(n)
-            if ok(s):
                 empty_tok(s, 0)
+                for n, j in mms[:cut]:
+                    matmul_out1(n, [j])
+                transpose_tok(s, 1)
                 empty_tok(s, 1)
-            for n in outs[:1]:
-                empty_out0(n)
-            for n in outs[1:]:
-                matmul_out0(n)
+            for q in at(pair_step, s - 1):
+                transpose_x0(q)
+                if X3_FIRST:
+                    group_x(q, 3)
+                empty_x0(q)
+                if not X3_FIRST:
+                    group_x(q, 3)
             if ok(s - 1):
                 quantize_tok(s - 1)
+            for n, j in mms[cut:]:
+                matmul_out1(n, [j])
+            for n in outs:
+                matmul_out0(n)
             if s == W_STEP:
                 group_w()
             for n in at(feat_step, s):
-                quantize_feat(n)
+                if not late:
+                    quantize_feat(n)
             if s == W_STEP:
                 quantize_w()
             for n in at(qf_step, s):
-                quantize_f(n)
-            for q in at(done, s):
-                if not (q % 2 == 0 or q - 1 not in at(done, s)):
-                    transpose_x0(q)
-                empty_x0(q)
-            for q, k in at(piece_step, s):
-                group_x(q, k)
-            for n in outs[1:]:
+                if mm_step[n] != s:
+                    quantize_f(n)
+            for n in at(feat_step, s):
+                if late:
+                    group_feat(n)
+            for n in at(feat_step, s - 1):
+                if s - 1 >= UNITS - F_DEFER:
+                    quantize_feat(n)
+                    matmul_out0(n)
+                    outs = outs + [n]
+            for q in at(pair_step, s):
+                group_x(q, 2)
+                group_x(q, 1)
+            if s == mm_step[UNITS - 1] and OUT1_FIRST:
+                finish_out1()
+            for n in outs:
                 empty_out0(n)
-            if s == done[1]:
-                go_late(0, 2)
-                load_x(2, 2)
-                load_x(1, 2)
-                go_late(1, 2)
-                load_x0(0, 1)
-                load_x(3, 2)
-                go_late(2, 2)
-                load_x0(1, 1)
-                go_late(3, 2)
-            if s == done[3]:
-                load_x(2, 3)
-                go_late(0, 3)
-                load_x(1, 3)
-                load_x(3, 3)
-                go_late(1, 3)
-                go_late(2, 3)
-                go_late(3, 3)
+            if s == pair_step[1] + 1:
+                load_group(2)
+            if s == pair_step[3] + 1:
+                load_group(3)
             if s == STORE_STEP:
                 for b in range(B):
                     store_out0(b, 0)
             for n in range(UNITS // 2, UNITS):
                 if max(STORE_STEP, out0_step[n]) == s:
                     store_out0(n % B, n // B)
-            if s == mm_step[UNITS - 1]:
+            if s == mm_step[UNITS - 1] and not OUT1_FIRST:
                 finish_out1()

@@ -24,10 +24,10 @@ PAIRS = UNITS // 2
 X_START = 1
 CATCH_UP = (9, 12)
 F_DEFER = 1
-W_STEP = 4
+W_STEP = 1
 FEAT_BUFS = 6
 TOK_BUFS = 4
-V_SHARE = {q: (1, 3) if q == PAIRS - 1 else (1,) for q in range(PAIRS)}
+V_SHARE = {q: (1,) for q in range(PAIRS)}
 ORDER0 = [(2, 0), (2, 1), (1, 0), (3, 0), (1, 1), (3, 1)]
 ORDER = [(2, 0), (1, 0), (3, 0), (2, 1), (1, 1), (3, 1)]
 X_NUM, X_OFF, X_DEN = 7, 6, 12
@@ -35,9 +35,28 @@ X0_STEP = 4
 STORE_STEP = 11
 Q_LAG = 2
 Q_ODD = 1
-M_LAG = 3
-HALVES = True
-LEAD1 = 9
+M_LAG = 2
+HALVES = False
+SEQ0 = [("go", 0), ("x", 2), ("x", 1), ("go", 1), ("go", 2), ("x", 3), ("x0", 0), ("go", 3), ("x0", 1)]
+SEQ = [("go", 0), ("x", 2), ("x", 1), ("go", 1), ("x", 3), ("x0", 0), ("go", 2), ("go", 3), ("x0", 1)]
+MODE = 2
+I_LATE0 = 1
+TAILV = 0
+DEFER = 1
+FEAT_RAW = 3
+M_BEFORE = ()
+X0_0 = {0: 2}
+QF_0 = {}
+O_RATE = 2
+O_HOLD = 0
+X1_0 = {1: 1}
+X2_0 = {1: 1}
+X3_0 = {}
+JM = 2
+Q_AFTER = 1
+O15_V = False
+
+LEAD1 = 7
 LEAD2 = 9
 TIGHT = 0
 X3_FIRST = True
@@ -45,14 +64,14 @@ OUT1_FIRST = False
 X0_BUFS = 4
 M_FIRST = False
 AHEAD = 0
-W_POS = 9
+W_POS = 4
 SPLIT = True
 GI_S = ()
 OUT1_V = ()
 JOIN = True
 F_SHIFT = 2
 X_BUFS = 2
-FP_BUFS = 3
+FP_BUFS = 4
 GO_BUFS = 8
 FQ_BUFS = 5
 LOADS = [("go", 0, 0), ("x", 2, 0), ("go", 1, 0), ("x", 1, 0), ("go", 2, 0), ("go", 3, 0), ("x", 3, 0), ("x0", 0, 0), ("go", 0, 1), "w",
@@ -133,7 +152,7 @@ def tile_graph_conv_pb_v_kernel(tc, x0, x1, x2, laplacian, weight, bias, x3, gra
         feat, feat_q, tok, tok_q, f_pair, f_q, banks, staged = {}, {}, {}, {}, {}, {}, {}, {}
 
         def group_feat(n):
-            t = work.tile([P, PASS, PACK], BF16, name="feat", bufs=2, align_bytes=64)
+            t = work.tile([P, PASS, PACK], BF16, name="feat", bufs=FEAT_RAW, align_bytes=64)
             dst = t[:].rearrange("p (h c i) t -> p h c t i", h=2, i=4)
             src = go[dz_bg(n)].rearrange("p t (h c i) -> p h c t i", h=2, i=4)
             if n in GI_S:
@@ -169,7 +188,10 @@ def tile_graph_conv_pb_v_kernel(tc, x0, x1, x2, laplacian, weight, bias, x3, gra
                     t = loads.tile([P, PASS], F32, name="staged_late", tag="go_unit", bufs=GO_BUFS, align_bytes=64)
                 staged[b, g] = t[:]
             dst = staged[b, 0][:, g * PASS:(g + 1) * PASS] if g < 2 else staged[b, g]
-            nc.scalar.copy(out=dst, in_=banks["out0", n])
+            if O15_V and n == UNITS - 1:
+                nc.vector.tensor_copy(out=dst, in_=banks["out0", n])
+            else:
+                nc.scalar.copy(out=dst, in_=banks["out0", n])
 
         def store_out0(b, g):
             width = 2 * PASS if g == 0 else PASS
@@ -218,8 +240,8 @@ def tile_graph_conv_pb_v_kernel(tc, x0, x1, x2, laplacian, weight, bias, x3, gra
                 dst = pair_tile(q).rearrange("p (bl k c t) -> p k c t bl", bl=2, k=K, t=PACK)
                 src = xs[k, g].rearrange("p j (c bh bl) -> p bh c j bl", bh=2, bl=2)
             else:
-                dst = pair_tile(q).rearrange("p (bl k c i t) -> p k c t i bl", bl=2, k=K, i=2, t=PACK)
-                src = xs[k, g].rearrange("p j (c i bh bl) -> p bh c j i bl", i=2, bh=2, bl=2)
+                dst = pair_tile(q).rearrange("p (bl k c i t) -> p k c t bl i", bl=2, k=K, i=2, t=PACK)
+                src = xs[k, g].rearrange("p j (c i bh bl) -> p bh c j bl i", i=2, bh=2, bl=2)
             if k in V_SHARE.get(q, ()):
                 nc.vector.tensor_copy(out=dst[:, k], in_=src[:, bh])
             else:
@@ -254,9 +276,7 @@ def tile_graph_conv_pb_v_kernel(tc, x0, x1, x2, laplacian, weight, bias, x3, gra
 
         def load_group(g):
             halves = HALVES and g >= 2
-            seq = [("go", 0), ("x", 2), ("x", 1), ("go", 1), ("x", 3), ("x0", 0), ("go", 2), ("go", 3), ("x0", 1)]
-            if g == 0:
-                seq = seq[:W_POS] + [("w", 0)] + seq[W_POS:]
+            seq = SEQ0[:W_POS] + [("w", 0)] + SEQ0[W_POS:] if g == 0 else SEQ
             for kind, i in seq:
                 if kind == "w":
                     load_w()
@@ -274,85 +294,104 @@ def tile_graph_conv_pb_v_kernel(tc, x0, x1, x2, laplacian, weight, bias, x3, gra
 
         load_group(0)
         load_group(1)
-        feat_step = {n: n + (F_SHIFT if n >= UNITS - F_DEFER else 0) for n in range(UNITS)}
-        out0_step = {n: max(feat_step[n] + 1, W_STEP + 1 + n // 2) for n in range(UNITS)}
+        out0_step = {n: max(n + 1, W_STEP + 1 + n // O_RATE) for n in range(UNITS - DEFER)}
         pair_step = {q: 2 * q - (q >= LEAD1) - (q >= LEAD2) for q in range(PAIRS)}
-        qf_step = {n: pair_step[n // 2] + 2 + n % 2 for n in range(UNITS)}
-        mm_step = {n: max(qf_step[n] + (1 if n >= TIGHT else 0), min(n + M_LAG, UNITS + 1)) for n in range(UNITS)}
-        mm_step[UNITS - 2] = min(mm_step[UNITS - 2], UNITS + 1) if JOIN else mm_step[UNITS - 2]
-        mm_step[UNITS - 1] = min(mm_step[UNITS - 1], UNITS + 1) if JOIN else mm_step[UNITS - 1]
-        last = max(max(out0_step.values()), max(mm_step.values()))
+        x0_step = {q: X0_0.get(q, pair_step[q] + 1) for q in range(PAIRS)}
+        x1_step = {q: X1_0.get(q, pair_step[q]) for q in range(PAIRS)}
+        x2_step = {q: X2_0.get(q, pair_step[q]) for q in range(PAIRS)}
+        x3_step = {q: X3_0.get(q, x0_step[q]) for q in range(PAIRS)}
+        qf_step = {n: QF_0.get(n, pair_step[n // 2] + 2 + n % 2) for n in range(UNITS)}
+        mm_step = {n: max(qf_step[n] + 1, n + M_LAG) for n in range(UNITS)}
 
         def at(table, s):
             return [key for key in table if table[key] == s]
 
-        for s in range(last + 1):
-            outs = [n for n in at(out0_step, s) if feat_step[n] < UNITS - F_DEFER]
+        for s in range(UNITS):
+            outs = at(out0_step, s)
             mms = [(n, j) for n in at(mm_step, s) for j in range(PACK)]
-            cut = len(mms) // 2 if SPLIT and ok(s) else 0
-            for n in at(qf_step, s):
-                if mm_step[n] == s:
-                    quantize_f(n)
-            late = s >= UNITS - F_DEFER
-            if s == mm_step[UNITS - 1]:
-                mms = sorted(mms, key=lambda nj: nj[1])
-            for n in at(feat_step, s):
-                if not late:
-                    group_feat(n)
-            if ok(s):
-                transpose_tok(s, 0)
-                empty_tok(s, 0)
-                for n, j in mms[:cut]:
+            x0s_now = at(x0_step, s)
+            cut = len(mms) // 2 if MODE == 1 else 0
+            cut2 = len(mms) // 2 if MODE == 2 and x0s_now else cut
+            if s in M_BEFORE:
+                for n, j in mms:
                     matmul_out1(n, [j])
-                transpose_tok(s, 1)
-                empty_tok(s, 1)
-            for q in at(pair_step, s - 1):
+                mms = []
+                cut = cut2 = 0
+            if s < UNITS - DEFER:
+                group_feat(s)
+            transpose_tok(s, 0)
+            empty_tok(s, 0)
+            for n, j in mms[:cut]:
+                matmul_out1(n, [j])
+            transpose_tok(s, 1)
+            empty_tok(s, 1)
+            for n, j in mms[cut:cut2]:
+                matmul_out1(n, [j])
+            for q in x0s_now:
                 transpose_x0(q)
+            for q in at(x3_step, s):
                 if X3_FIRST:
                     group_x(q, 3)
+            for q in x0s_now:
                 empty_x0(q)
+            for q in at(x3_step, s):
                 if not X3_FIRST:
                     group_x(q, 3)
             if ok(s - 1):
                 quantize_tok(s - 1)
-            for n, j in mms[cut:]:
+            for n, j in mms[cut2:]:
                 matmul_out1(n, [j])
             for n in outs:
                 matmul_out0(n)
             if s == W_STEP:
                 group_w()
-            for n in at(feat_step, s):
-                if not late:
-                    quantize_feat(n)
+            if s < UNITS - DEFER:
+                quantize_feat(s)
             if s == W_STEP:
                 quantize_w()
             for n in at(qf_step, s):
-                if mm_step[n] != s:
-                    quantize_f(n)
-            for n in at(feat_step, s):
-                if late:
-                    group_feat(n)
-            for n in at(feat_step, s - 1):
-                if s - 1 >= UNITS - F_DEFER:
-                    quantize_feat(n)
-                    matmul_out0(n)
-                    outs = outs + [n]
-            for q in at(pair_step, s):
+                quantize_f(n)
+            for q in at(x2_step, s):
                 group_x(q, 2)
+            for q in at(x1_step, s):
                 group_x(q, 1)
-            if s == mm_step[UNITS - 1] and OUT1_FIRST:
-                finish_out1()
             for n in outs:
-                empty_out0(n)
-            if s == pair_step[1] + 1:
+                if n < UNITS - 1 - O_HOLD or s == UNITS - 1:
+                    empty_out0(n)
+            if s == UNITS - 1:
+                for n in range(UNITS - 1 - O_HOLD, UNITS - 2):
+                    empty_out0(n)
+                    store_out0(n % B, n // B)
+            if s == max(x0_step[1], x3_step[1]):
                 load_group(2)
-            if s == pair_step[3] + 1:
+            if s == x0_step[3]:
                 load_group(3)
             if s == STORE_STEP:
                 for b in range(B):
                     store_out0(b, 0)
-            for n in range(UNITS // 2, UNITS):
-                if max(STORE_STEP, out0_step[n]) == s:
+            for n in range(UNITS // 2, UNITS - DEFER):
+                if max(STORE_STEP, out0_step[n]) == s and (n < UNITS - 1 - O_HOLD or s == UNITS - 1):
                     store_out0(n % B, n // B)
-            if s == mm_step[UNITS - 1] and not OUT1_FIRST:
-                finish_out1()
+
+        last = UNITS - 1
+        late = list(range(UNITS - DEFER, UNITS))
+        for n in late[:TAILV]:
+            group_feat(n)
+        rest_q = [n for n in range(UNITS) if qf_step[n] >= UNITS]
+        for n in rest_q:
+            quantize_f(n)
+        quantize_tok(last)
+        rest_m = [n for n in range(UNITS) if mm_step[n] >= UNITS]
+        for n in rest_m[:-JM]:
+            matmul_out1(n, range(PACK))
+        for j in range(PACK):
+            for n in rest_m[-JM:]:
+                matmul_out1(n, [j])
+        for n in late[TAILV:]:
+            group_feat(n)
+        finish_out1()
+        for n in late:
+            quantize_feat(n)
+            matmul_out0(n)
+            empty_out0(n)
+            store_out0(n % B, n // B)

@@ -38,10 +38,12 @@ Q_ODD = 1
 M_LAG = 2
 HALVES = False
 SEQ0 = [("go", 0), ("x", 2), ("x", 1), ("go", 1), ("go", 2), ("x", 3), ("x0", 0), ("go", 3), ("x0", 1)]
-SEQ = [("go", 0), ("x", 2), ("x", 1), ("go", 1), ("x", 3), ("x0", 0), ("go", 2), ("go", 3), ("x0", 1)]
+SEQ = [("x", 1), ("go", 0), ("x", 2), ("go", 1), ("x", 3), ("x0", 0), ("go", 2), ("go", 3), ("x0", 1)]
 MODE = 2
 I_LATE0 = 1
 TAILV = 0
+X1_ODD = -1
+X1_FIRST = False
 DEFER = 1
 FEAT_RAW = 3
 M_BEFORE = ()
@@ -49,14 +51,14 @@ X0_0 = {0: 2}
 QF_0 = {}
 O_RATE = 2
 O_HOLD = 0
-X1_0 = {1: 1}
+X1_0 = {0: 0, 1: 1}
 X2_0 = {1: 1}
 X3_0 = {}
 JM = 2
 Q_AFTER = 1
 O15_V = False
 
-LEAD1 = 7
+LEAD1 = 5
 LEAD2 = 9
 TIGHT = 0
 X3_FIRST = True
@@ -159,8 +161,8 @@ def tile_graph_conv_pb_v_kernel(tc, x0, x1, x2, laplacian, weight, bias, x3, gra
                 nc.vector.tensor_copy(out=dst[:, 0], in_=src[:, 0])
                 nc.scalar.copy(out=dst[:, 1], in_=src[:, 1])
             else:
-                nc.vector.tensor_copy(out=t[:].rearrange("p (c i) t -> p c t i", i=4),
-                                      in_=go[dz_bg(n)].rearrange("p t (c i) -> p c t i", i=4))
+                nc.vector.tensor_copy(out=t[:].rearrange("p (c i) t -> p c t i", i=2),
+                                      in_=go[dz_bg(n)].rearrange("p t (c i) -> p c t i", i=2))
             feat[n] = t[:]
 
         def quantize(src, fmt, name, bufs):
@@ -240,8 +242,8 @@ def tile_graph_conv_pb_v_kernel(tc, x0, x1, x2, laplacian, weight, bias, x3, gra
                 dst = pair_tile(q).rearrange("p (bl k c t) -> p k c t bl", bl=2, k=K, t=PACK)
                 src = xs[k, g].rearrange("p j (c bh bl) -> p bh c j bl", bh=2, bl=2)
             else:
-                dst = pair_tile(q).rearrange("p (bl k c i t) -> p k c t bl i", bl=2, k=K, i=2, t=PACK)
-                src = xs[k, g].rearrange("p j (c i bh bl) -> p bh c j bl i", i=2, bh=2, bl=2)
+                dst = pair_tile(q).rearrange("p (bl k c i t) -> p k c bl t i", bl=2, k=K, i=2, t=PACK)
+                src = xs[k, g].rearrange("p j (c i bh bl) -> p bh c bl j i", i=2, bh=2, bl=2)
             if k in V_SHARE.get(q, ()):
                 nc.vector.tensor_copy(out=dst[:, k], in_=src[:, bh])
             else:
@@ -297,7 +299,7 @@ def tile_graph_conv_pb_v_kernel(tc, x0, x1, x2, laplacian, weight, bias, x3, gra
         out0_step = {n: max(n + 1, W_STEP + 1 + n // O_RATE) for n in range(UNITS - DEFER)}
         pair_step = {q: 2 * q - (q >= LEAD1) - (q >= LEAD2) for q in range(PAIRS)}
         x0_step = {q: X0_0.get(q, pair_step[q] + 1) for q in range(PAIRS)}
-        x1_step = {q: X1_0.get(q, pair_step[q]) for q in range(PAIRS)}
+        x1_step = {q: X1_0.get(q, pair_step[q] + X1_ODD) for q in range(PAIRS)}
         x2_step = {q: X2_0.get(q, pair_step[q]) for q in range(PAIRS)}
         x3_step = {q: X3_0.get(q, x0_step[q]) for q in range(PAIRS)}
         qf_step = {n: QF_0.get(n, pair_step[n // 2] + 2 + n % 2) for n in range(UNITS)}
@@ -351,10 +353,14 @@ def tile_graph_conv_pb_v_kernel(tc, x0, x1, x2, laplacian, weight, bias, x3, gra
                 quantize_w()
             for n in at(qf_step, s):
                 quantize_f(n)
+            for q in at(x1_step, s):
+                if X1_FIRST:
+                    group_x(q, 1)
             for q in at(x2_step, s):
                 group_x(q, 2)
             for q in at(x1_step, s):
-                group_x(q, 1)
+                if not X1_FIRST:
+                    group_x(q, 1)
             for n in outs:
                 if n < UNITS - 1 - O_HOLD or s == UNITS - 1:
                     empty_out0(n)

from contextlib import ExitStack

import concourse.mybir as mybir
from concourse.masks import make_identity

B, C, V, K, OUT = 4, 128, 2048, 4, 512
FLOPS = 2 * B * V * OUT * C + 2 * B * V * OUT * C * K
BYTES = 2 * (B * C * V + 2 * V * C * B + OUT * C * K + B * OUT * V) + 4 * (V * C * B + B * C * V + OUT * C * K)

F32 = mybir.dt.float32
BF16 = mybir.dt.bfloat16
U32 = mybir.dt.uint32
U8 = mybir.dt.uint8
E4M3 = mybir.dt.float8_e4m3fn_x4
E5M2 = mybir.dt.float8_e5m2_x4

P = 128
PACK = 4
PASS = P * PACK
GROUPS = V // PASS
UNITS = B * GROUPS
PAIRS = UNITS // 2

X_START = 1
CATCH_UP = (9, 12)
F_DEFER = 1
W_STEP = 1
FEAT_BUFS = 6
TOK_BUFS = 4
V_SHARE = {q: (1,) for q in range(PAIRS)}
ORDER0 = [(2, 0), (2, 1), (1, 0), (3, 0), (1, 1), (3, 1)]
ORDER = [(2, 0), (1, 0), (3, 0), (2, 1), (1, 1), (3, 1)]
X_NUM, X_OFF, X_DEN = 7, 6, 12
X0_STEP = 4
STORE_STEP = 11
Q_LAG = 2
Q_ODD = 1
M_LAG = 2
HALVES = False
SEQ0 = [("go", 0), ("x", 2), ("x", 1), ("go", 1), ("go", 2), ("x", 3), ("x0", 0), ("go", 3), ("x0", 1)]
SEQ = [("x", 1), ("go", 0), ("x", 2), ("go", 1), ("x", 3), ("x0", 0), ("go", 2), ("go", 3), ("x0", 1)]
MODE = 2
I_LATE0 = 1
TAILV = 0
X1_ODD = -1
X1_FIRST = False
DEFER = 1
FEAT_RAW = 3
M_BEFORE = ()
X0_0 = {0: 2}
QF_0 = {}
O_RATE = 2
O_HOLD = 0
X1_0 = {0: 0, 1: 1}
X2_0 = {1: 1}
X3_0 = {}
JM = 2
Q_AFTER = 1
O15_V = False

LEAD1 = 5
LEAD2 = 9
TIGHT = 0
X3_FIRST = True
OUT1_FIRST = False
X0_BUFS = 4
M_FIRST = False
AHEAD = 0
W_POS = 4
SPLIT = True
GI_S = ()
OUT1_V = ()
JOIN = True
F_SHIFT = 2
X_BUFS = 2
FP_BUFS = 4
GO_BUFS = 8
FQ_BUFS = 5
LOADS = [("go", 0, 0), ("x", 2, 0), ("go", 1, 0), ("x", 1, 0), ("go", 2, 0), ("go", 3, 0), ("x", 3, 0), ("x0", 0, 0), ("go", 0, 1), "w",
         ("x0", 1, 0), ("go", 1, 1), ("x", 2, 1), ("x", 1, 1), ("go", 2, 1), ("x", 3, 1), ("go", 3, 1)]


def dz_bg(n):
    return n % B, n // B


def x_step(i):
    return X_START + i - sum(1 for c in CATCH_UP if i >= c)


def tile_graph_conv_pb_v_kernel(tc, x0, x1, x2, laplacian, weight, bias, x3, grad_out, out_0, out_1):
    nc = tc.nc
    with ExitStack() as ctx:
        keep = ctx.enter_context(tc.tile_pool(name="keep", bufs=1))
        loads = ctx.enter_context(tc.tile_pool(name="loads", bufs=2))
        work = ctx.enter_context(tc.tile_pool(name="work", bufs=2))
        psum = ctx.enter_context(tc.psum_pool(name="psum", bufs=1))
        ctx.enter_context(tc.manual_schedule())

        ident = keep.tile([P, P], F32, name="ident")
        make_identity(nc, ident[:])

        go, xs, x0s = {}, {}, {}

        def load_go_unit(b, g):
            t = loads.tile([P, PACK, PASS], BF16, name="go_unit", tag="go_unit", bufs=GO_BUFS, align_bytes=64)
            src = grad_out[b].rearrange("(p j) v -> p j v", j=PACK)
            nc.sync.dma_start(out=t[:], in_=src[:, :, g * PASS:(g + 1) * PASS])
            go[b, g] = t[:]

        def load_go_half(b, half):
            t = loads.tile([P, PACK, 2 * PASS], BF16, name="go_half", bufs=4, align_bytes=64)
            src = grad_out[b].rearrange("(p j) v -> p j v", j=PACK)
            nc.sync.dma_start(out=t[:], in_=src[:, :, 2 * half * PASS:2 * (half + 1) * PASS])
            go[b, 2 * half] = t[:, :, 0:PASS]
            go[b, 2 * half + 1] = t[:, :, PASS:2 * PASS]

        def load_x(k, g):
            src = (x1, x2, x3)[k - 1]
            t = loads.tile([P, PACK, C * B], F32 if k == 3 else BF16, name="x%d" % k, bufs=X_BUFS, align_bytes=64)
            nc.sync.dma_start(out=t[:], in_=src[g * PASS:(g + 1) * PASS, :].rearrange("(p j) w -> p j w", j=PACK))
            xs[k, g] = t[:]

        def load_x0(bh, half):
            t = loads.tile([P, 2, 2 * PASS], BF16, name="x0", tag="x0", bufs=2, align_bytes=64)
            src = x0[2 * bh:2 * bh + 2, :, 2 * half * PASS:2 * (half + 1) * PASS]
            nc.sync.dma_start(out=t[:], in_=src.rearrange("b c v -> c b v"))
            x0s[bh, 2 * half] = t[:, :, 0:PASS]
            x0s[bh, 2 * half + 1] = t[:, :, PASS:2 * PASS]

        def load_x0_pair(bh, g):
            t = loads.tile([P, 2, PASS], BF16, name="x0p", tag="x0p", bufs=X0_BUFS, align_bytes=64)
            nc.sync.dma_start(out=t[:], in_=x0[2 * bh:2 * bh + 2, :, g * PASS:(g + 1) * PASS].rearrange("b c v -> c b v"))
            x0s[bh, g] = t[:]

        w_raw = keep.tile([P, PACK, C * K], BF16, name="w_raw")
        w_grouped = keep.tile([P, C, PACK], BF16, name="w_grouped", align_bytes=64)
        w_codes = keep.tile([P, C], U32, name="w_codes", align_bytes=64)
        w_scales = keep.tile([P, C], U8, name="w_scales", align_bytes=64)

        def load_w():
            nc.sync.dma_start(out=w_raw[:], in_=weight.rearrange("(p j) w -> p j w", j=PACK))

        def group_w():
            src = w_raw[:].rearrange("p j (c k) -> p k c j", k=K)
            nc.vector.tensor_copy(out=w_grouped[:], in_=src[:, 0])

        def quantize_w():
            nc.vector.quantize_mx(out=w_codes[:].bitcast(E4M3), scales=w_scales[:],
                                  in_=w_grouped[:].rearrange("p c j -> p (c j)"))

        acc = [psum.tile([P, PASS], F32, name="acc%d" % j) for j in range(PACK)]

        feat, feat_q, tok, tok_q, f_pair, f_q, banks, staged = {}, {}, {}, {}, {}, {}, {}, {}

        def group_feat(n):
            t = work.tile([P, PASS, PACK], BF16, name="feat", bufs=FEAT_RAW, align_bytes=64)
            dst = t[:].rearrange("p (h c i) t -> p h c t i", h=2, i=4)
            src = go[dz_bg(n)].rearrange("p t (h c i) -> p h c t i", h=2, i=4)
            if n in GI_S:
                nc.vector.tensor_copy(out=dst[:, 0], in_=src[:, 0])
                nc.scalar.copy(out=dst[:, 1], in_=src[:, 1])
            else:
                nc.vector.tensor_copy(out=t[:].rearrange("p (c i) t -> p c t i", i=2),
                                      in_=go[dz_bg(n)].rearrange("p t (c i) -> p c t i", i=2))
            feat[n] = t[:]

        def quantize(src, fmt, name, bufs):
            codes = work.tile([P, PASS], U32, name=name + "_codes", bufs=bufs, align_bytes=64)
            scales = work.tile([P, PASS], U8, name=name + "_scales", bufs=bufs, align_bytes=64)
            nc.vector.quantize_mx(out=codes[:].bitcast(fmt), scales=scales[:], in_=src)
            return codes[:], scales[:]

        def quantize_feat(n):
            feat_q[n] = quantize(feat[n].rearrange("p v j -> p (v j)"), E5M2, "feat", FEAT_BUFS)

        def matmul_out0(n):
            bank = psum.tile([P, PASS], F32, name="bank_out0", tag="bank", bufs=4)
            codes, scales = feat_q[n]
            nc.tensor.matmul_mx(out=bank[:], lhsT=w_codes[:].bitcast(E4M3), lhsT_scale=w_scales[:],
                                rhs=codes.bitcast(E5M2), rhs_scale=scales, start=True, stop=True)
            banks["out0", n] = bank[:]

        def empty_out0(n):
            b, g = dz_bg(n)
            if g != 1:
                if g == 0:
                    t = keep.tile([P, 2 * PASS], F32, name="staged_%d" % b)
                else:
                    t = loads.tile([P, PASS], F32, name="staged_late", tag="go_unit", bufs=GO_BUFS, align_bytes=64)
                staged[b, g] = t[:]
            dst = staged[b, 0][:, g * PASS:(g + 1) * PASS] if g < 2 else staged[b, g]
            if O15_V and n == UNITS - 1:
                nc.vector.tensor_copy(out=dst, in_=banks["out0", n])
            else:
                nc.scalar.copy(out=dst, in_=banks["out0", n])

        def store_out0(b, g):
            width = 2 * PASS if g == 0 else PASS
            nc.sync.dma_start(out=out_0[b, :, g * PASS:g * PASS + width], in_=staged[b, g])

        def transpose_tok(n, jh):
            bank = psum.tile([P, 2, 2, P], F32, name="bank_tr", tag="bank", bufs=4)
            words = go[dz_bg(n)].bitcast(F32)
            for jl in range(2):
                for u in range(2):
                    nc.tensor.transpose(bank[:, jl, u, :], words[:, 2 * jh + jl, u:PASS // 2:2], ident[:])
            banks["tok", n, jh] = bank[:]

        def empty_tok(n, jh):
            if jh == 0:
                t = work.tile([P, 2, PASS], F32, name="tok", bufs=2, align_bytes=64)
                tok[n] = t[:]
            nc.scalar.copy(out=tok[n][:, jh, :].rearrange("p (j r u) -> p j r u", j=2, u=2),
                           in_=banks["tok", n, jh].rearrange("p j u r -> p j r u"))

        def quantize_tok(n):
            tok_q[dz_bg(n)] = quantize(tok[n].rearrange("p h w -> p (h w)").bitcast(BF16), E5M2, "tok", TOK_BUFS)

        def pair_tile(q):
            if q not in f_pair:
                t = work.tile([P, 2 * K * C * PACK], BF16, name="f_pair", bufs=FP_BUFS, align_bytes=64)
                f_pair[q] = t[:]
            return f_pair[q]

        def transpose_x0(q):
            g, bh = divmod(q, 2)
            bank = psum.tile([P, 2, 2, P], F32, name="bank_tr", tag="bank", bufs=4)
            words = x0s[bh, g].bitcast(F32)
            for bl in range(2):
                for u in range(2):
                    nc.tensor.transpose(bank[:, bl, u, :], words[:, bl, u:PASS // 2:2], ident[:])
            banks["x0", q] = bank[:]

        def empty_x0(q):
            dst = pair_tile(q).bitcast(F32).rearrange("p (bl k c u) -> p k bl c u", bl=2, k=K, u=2)
            nc.scalar.copy(out=dst[:, 0], in_=banks["x0", q].rearrange("p bl u c -> p bl c u"))

        def group_x(q, k):
            g, bh = divmod(q, 2)
            if k == 3:
                dst = pair_tile(q).rearrange("p (bl k c t) -> p k c t bl", bl=2, k=K, t=PACK)
                src = xs[k, g].rearrange("p j (c bh bl) -> p bh c j bl", bh=2, bl=2)
            else:
                dst = pair_tile(q).rearrange("p (bl k c i t) -> p k c bl t i", bl=2, k=K, i=2, t=PACK)
                src = xs[k, g].rearrange("p j (c i bh bl) -> p bh c bl j i", i=2, bh=2, bl=2)
            if k in V_SHARE.get(q, ()):
                nc.vector.tensor_copy(out=dst[:, k], in_=src[:, bh])
            else:
                nc.scalar.copy(out=dst[:, k], in_=src[:, bh])

        def quantize_f(n):
            width = K * C * PACK
            f_q[n] = quantize(f_pair[n // 2][:, (n % 2) * width:(n % 2 + 1) * width], E4M3, "f", FQ_BUFS)

        def matmul_out1(n, js):
            dz_codes, dz_scales = tok_q[n % B, n // B]
            f_codes, f_scales = f_q[n]
            for j in js:
                cols = slice(j * P, (j + 1) * P)
                nc.tensor.matmul_mx(out=acc[j][:], lhsT=dz_codes[:, cols].bitcast(E5M2), lhsT_scale=dz_scales[:, cols],
                                    rhs=f_codes.bitcast(E4M3), rhs_scale=f_scales,
                                    start=(n == 0), stop=(n == UNITS - 1))

        def finish_out1():
            rows = out_1.rearrange("(p j) w -> p j w", j=PACK)
            for j in range(PACK):
                t = loads.tile([P, C, K], F32, name="dw", tag="x0p", bufs=X0_BUFS, align_bytes=64)
                src = acc[j][:].rearrange("p (k c) -> p c k", k=K)
                if j in OUT1_V:
                    nc.vector.tensor_copy(out=t[:], in_=src)
                else:
                    nc.scalar.copy(out=t[:], in_=src)
                nc.sync.dma_start(out=rows[:, j, :], in_=t[:].rearrange("p c k -> p (c k)"))

        def ok(n, count=UNITS):
            return 0 <= n < count

        def load_group(g):
            halves = HALVES and g >= 2
            seq = SEQ0[:W_POS] + [("w", 0)] + SEQ0[W_POS:] if g == 0 else SEQ
            for kind, i in seq:
                if kind == "w":
                    load_w()
                elif kind == "x":
                    load_x(i, g)
                elif kind == "go":
                    if not halves:
                        load_go_unit(i, g)
                    elif g == 2:
                        load_go_half(i, 1)
                elif not halves:
                    load_x0_pair(i, g)
                elif g == 2:
                    load_x0(i, 1)

        load_group(0)
        load_group(1)
        out0_step = {n: max(n + 1, W_STEP + 1 + n // O_RATE) for n in range(UNITS - DEFER)}
        pair_step = {q: 2 * q - (q >= LEAD1) - (q >= LEAD2) for q in range(PAIRS)}
        x0_step = {q: X0_0.get(q, pair_step[q] + 1) for q in range(PAIRS)}
        x1_step = {q: X1_0.get(q, pair_step[q] + X1_ODD) for q in range(PAIRS)}
        x2_step = {q: X2_0.get(q, pair_step[q]) for q in range(PAIRS)}
        x3_step = {q: X3_0.get(q, x0_step[q]) for q in range(PAIRS)}
        qf_step = {n: QF_0.get(n, pair_step[n // 2] + 2 + n % 2) for n in range(UNITS)}
        mm_step = {n: max(qf_step[n] + 1, n + M_LAG) for n in range(UNITS)}

        def at(table, s):
            return [key for key in table if table[key] == s]

        for s in range(UNITS):
            outs = at(out0_step, s)
            mms = [(n, j) for n in at(mm_step, s) for j in range(PACK)]
            x0s_now = at(x0_step, s)
            cut = len(mms) // 2 if MODE == 1 else 0
            cut2 = len(mms) // 2 if MODE == 2 and x0s_now else cut
            if s in M_BEFORE:
                for n, j in mms:
                    matmul_out1(n, [j])
                mms = []
                cut = cut2 = 0
            if s < UNITS - DEFER:
                group_feat(s)
            transpose_tok(s, 0)
            empty_tok(s, 0)
            for n, j in mms[:cut]:
                matmul_out1(n, [j])
            transpose_tok(s, 1)
            empty_tok(s, 1)
            for n, j in mms[cut:cut2]:
                matmul_out1(n, [j])
            for q in x0s_now:
                transpose_x0(q)
            for q in at(x3_step, s):
                if X3_FIRST:
                    group_x(q, 3)
            for q in x0s_now:
                empty_x0(q)
            for q in at(x3_step, s):
                if not X3_FIRST:
                    group_x(q, 3)
            if ok(s - 1):
                quantize_tok(s - 1)
            for n, j in mms[cut2:]:
                matmul_out1(n, [j])
            for n in outs:
                matmul_out0(n)
            if s == W_STEP:
                group_w()
            if s < UNITS - DEFER:
                quantize_feat(s)
            if s == W_STEP:
                quantize_w()
            for n in at(qf_step, s):
                quantize_f(n)
            for q in at(x1_step, s):
                if X1_FIRST:
                    group_x(q, 1)
            for q in at(x2_step, s):
                group_x(q, 2)
            for q in at(x1_step, s):
                if not X1_FIRST:
                    group_x(q, 1)
            for n in outs:
                if n < UNITS - 1 - O_HOLD or s == UNITS - 1:
                    empty_out0(n)
            if s == UNITS - 1:
                for n in range(UNITS - 1 - O_HOLD, UNITS - 2):
                    empty_out0(n)
                    store_out0(n % B, n // B)
            if s == max(x0_step[1], x3_step[1]):
                load_group(2)
            if s == x0_step[3]:
                load_group(3)
            if s == STORE_STEP:
                for b in range(B):
                    store_out0(b, 0)
            for n in range(UNITS // 2, UNITS - DEFER):
                if max(STORE_STEP, out0_step[n]) == s and (n < UNITS - 1 - O_HOLD or s == UNITS - 1):
                    store_out0(n % B, n // B)

        last = UNITS - 1
        late = list(range(UNITS - DEFER, UNITS))
        for n in late[:TAILV]:
            group_feat(n)
        rest_q = [n for n in range(UNITS) if qf_step[n] >= UNITS]
        for n in rest_q:
            quantize_f(n)
        quantize_tok(last)
        rest_m = [n for n in range(UNITS) if mm_step[n] >= UNITS]
        for n in rest_m[:-JM]:
            matmul_out1(n, range(PACK))
        for j in range(PACK):
            for n in rest_m[-JM:]:
                matmul_out1(n, [j])
        for n in late[TAILV:]:
            group_feat(n)
        finish_out1()
        for n in late:
            quantize_feat(n)
            matmul_out0(n)
            empty_out0(n)
            store_out0(n % B, n // B)
